import numpy as np
import ml_dtypes


def mxq(x, axis, fmt="e4m3"):
    dtype, down = {"e4m3": (ml_dtypes.float8_e4m3fn, 7), "e5m2": (ml_dtypes.float8_e5m2, 14)}[fmt]
    v = np.moveaxis(np.asarray(x, np.float32).astype(ml_dtypes.bfloat16).astype(np.float64), axis, -1)
    blocks = v.reshape(v.shape[:-1] + (-1, 32))
    amax = np.abs(blocks).max(-1, keepdims=True)
    byte = np.maximum(np.where(amax > 0, np.frexp(amax)[1] - 1 + 127, 0) - down, 1)
    scale = np.exp2(byte - 127.0)
    codes = (blocks / scale).astype(np.float32).astype(dtype).astype(np.float64)
    return np.moveaxis((codes * scale).reshape(v.shape), -1, axis)


WIDE = False


def mx_kscale(k):
    if not WIDE:
        return np.ones(k)
    levels = np.array([10, -10, 5, -5, 0])
    a = np.random.permutation(np.resize(levels, k // 512 * 4)).reshape(k // 512, 4)
    idx = np.arange(k)
    return np.exp2(a[idx // 512, idx % 128 // 32])


BF16 = ml_dtypes.bfloat16


def bf(x):
    return np.asarray(x, np.float32).astype(BF16)


def f64(x):
    return np.asarray(x).astype(np.float64)


E2M1 = np.array([0.0, 0.5, 1.0, 1.5, 2.0, 3.0, 4.0, 6.0, -0.0, -0.5, -1.0, -1.5, -2.0, -3.0, -4.0, -6.0])


def pack_weight(w, fmt):
    k, n = w.shape
    w = f64(bf(w)).reshape(k // 32, 32, n)
    amax = np.abs(w).max(1)
    if fmt == "e4m3":
        byte = np.frexp(amax)[1] - 1 + 127 - 7
    else:
        mant, ex = np.frexp(amax / 6.0)
        byte = np.where(mant > 0.5, ex, ex - 1) + 127
    byte = np.clip(np.where(amax > 0, byte, 1), 1, 254)
    scaled = (w * np.exp2(127.0 - byte)[:, None, :]).reshape(k, n).astype(np.float32)
    by_word = np.ascontiguousarray(scaled.reshape(k // 512, 128, 4, n).transpose(0, 1, 3, 2))
    if fmt == "e4m3":
        words = by_word.astype(ml_dtypes.float8_e4m3fn).view(np.uint8)
    else:
        c = by_word.astype(ml_dtypes.float4_e2m1fn).view(np.uint8) & 0xF
        words = c[..., 0::2] | (c[..., 1::2] << 4)
    return np.ascontiguousarray(words), np.ascontiguousarray(byte.astype(np.uint8).reshape(k // 512, 16, n))


def unpack_weight(words, scales, fmt):
    g, p, n, _ = words.shape
    if fmt == "e4m3":
        vals = np.ascontiguousarray(words).view(ml_dtypes.float8_e4m3fn).astype(np.float64)
    else:
        nib = np.empty((g, p, n, 4), np.uint8)
        nib[..., 0::2] = words & 0xF
        nib[..., 1::2] = words >> 4
        vals = E2M1[nib]
    vals = vals * np.repeat(np.exp2(scales.astype(np.float64) - 127.0), 8, axis=1)[..., None]
    return vals.transpose(0, 1, 3, 2).reshape(g * 512, n)

def pack4(w):
    words, scales = pack_weight(w, "e2m1")
    return words.reshape(words.shape[0], 128, -1), scales


def unpack4(words, scales):
    return unpack_weight(words.reshape(words.shape[0], 128, -1, 2), scales, "e2m1")


B, L, N, HID, H, D = 1, 128, 8192, 1024, 2, 64


def apply_rope(x, rope):
    xp = x.reshape(x.shape[:-1] + (D // 2, 2))
    rp = rope[:, None].reshape(rope.shape[0], 1, rope.shape[1], D // 2, 2)
    cos, sin = rp[..., 0], rp[..., 1]
    x0, x1 = xp[..., 0], xp[..., 1]
    out = np.stack([x0 * cos - x1 * sin, x1 * cos + x0 * sin], axis=-1)
    return out.reshape(x.shape)


def setup_inputs():
    s = mx_kscale(HID)
    img = bf(np.random.standard_normal((B, N, HID)) * s)
    rope = bf(np.random.standard_normal((B, N, D)))
    w = np.random.standard_normal((3 * H * D, HID)) / np.sqrt(HID) / s
    words, scales = pack4(np.ascontiguousarray(w.T))
    return {"img": img,
            "rope": rope,
            "W_img_qkv_words": words,
            "W_img_qkv_scales": scales}


def reference(img, rope, W_img_qkv_words, W_img_qkv_scales):
    y = mxq(f64(img), 2, "e4m3") @ unpack4(W_img_qkv_words, W_img_qkv_scales)
    y = y.reshape(B, N, 3, H, D).transpose(2, 0, 3, 1, 4)
    r = f64(rope)
    return apply_rope(y[0], r), apply_rope(y[1], r), y[2]

@@ -1,0 +1,233 @@
+from contextlib import ExitStack
+
+import concourse.mybir as mybir
+from concourse.masks import make_identity
+
+BF16 = mybir.dt.bfloat16
+F32 = mybir.dt.float32
+I32 = mybir.dt.int32
+U8 = mybir.dt.uint8
+U32 = mybir.dt.uint32
+FP8X4 = mybir.dt.float8_e4m3fn_x4
+FP4X4 = mybir.dt.float4_e2m1fn_x4
+MULT = mybir.AluOpType.mult
+ADD = mybir.AluOpType.add
+
+P = 128
+TOKENS = 8192
+K = 1024
+PACK = 4
+PASSES = K // (P * PACK)
+HEADS = 2
+D = 64
+HALF_D = D // 2
+COLS = 3 * HEADS * D
+BLOCK = HEADS * D
+TILES = TOKENS // P
+PAIR = 2
+ROUND = 4
+ROUNDS = TILES // ROUND
+LOAD_AHEAD = 4
+
+FLOPS = 2 * TOKENS * K * COLS
+
+
+def tile_jointattention_pa_t_kernel(
+    tc, img, rope, w_words, w_scales, out_q, out_k, out_v
+):
+    nc = tc.nc
+
+    img_v = img.rearrange("b (p t) k -> p (b t) k", t=TILES)
+    rope_v = rope.rearrange("b (p t) d -> p (b t) d", t=TILES)
+    out_q_v = out_q.rearrange("b h (p t) d -> p (b h) t d", t=TILES)
+    out_k_v = out_k.rearrange("b h (p t) d -> p (b h) t d", t=TILES)
+    out_v_v = out_v.rearrange("b h (p t) d -> p (b h) t d", t=TILES)
+
+    with ExitStack() as ctx:
+        const = ctx.enter_context(tc.tile_pool(name="const", bufs=1))
+        x_pool = ctx.enter_context(tc.tile_pool(name="x", bufs=LOAD_AHEAD + 2))
+        mx_pool = ctx.enter_context(tc.tile_pool(name="mx", bufs=2 * ROUND // PAIR))
+        table_pool = ctx.enter_context(tc.tile_pool(name="table", bufs=3))
+        res_pool = ctx.enter_context(tc.tile_pool(name="res", bufs=3))
+        xt_psum = ctx.enter_context(tc.psum_pool(name="xt_psum", bufs=ROUND))
+        qk_psum = ctx.enter_context(tc.psum_pool(name="qk_psum", bufs=ROUND // PAIR))
+        v_psum = ctx.enter_context(tc.psum_pool(name="v_psum", bufs=2))
+        ctx.enter_context(tc.manual_schedule())
+
+        x_tiles = {}
+        mx_tiles = {}
+        table_tiles = {}
+        res_tiles = {}
+
+        def load_round(r, pieces):
+            x_sb = x_pool.tile([P, ROUND, K], BF16, name="x_sb")
+            step = ROUND // pieces
+            for j in range(0, ROUND, step):
+                nc.sync.dma_start(
+                    out=x_sb[:, j : j + step, :],
+                    in_=img_v[:, r * ROUND + j : r * ROUND + j + step, :],
+                )
+            x_tiles[r] = x_sb
+
+        w_scale_sb = const.tile([P, PASSES, COLS], U8, align_bytes=64)
+        nc.vector.memset(w_scale_sb[:].bitcast(I32), 0)
+        ident = const.tile([P, P], F32)
+        make_identity(nc, ident[:])
+
+        load_round(0, ROUND)
+
+        w_code_sb = const.tile([P, PASSES, 2 * COLS], U8, align_bytes=64)
+        nc.sync.dma_start(
+            out=w_code_sb[:].bitcast(I32),
+            in_=w_words.rearrange("g p b -> p g b").bitcast(I32),
+        )
+        for quad in range(4):
+            nc.sync.dma_start(
+                out=w_scale_sb[32 * quad : 32 * quad + 4].bitcast(I32),
+                in_=w_scales[:, 4 * quad : 4 * quad + 4, :]
+                .rearrange("g r n -> r g n")
+                .bitcast(I32),
+            )
+        rope_sb = const.tile([P, TILES, D], BF16)
+        nc.sync.dma_start(out=rope_sb[:], in_=rope_v)
+        rope_pairs = rope_sb[:].rearrange("p t (i h) -> p t i h", h=2)
+        for r in range(1, LOAD_AHEAD):
+            load_round(r, 1)
+
+        def transpose_round(r):
+            words = x_tiles[r][:].bitcast(F32)
+            for half in range(ROUND // PAIR):
+                grouped = mx_pool.tile(
+                    [P, PAIR, PASSES, P, PACK], BF16, align_bytes=64, name="grouped"
+                )
+                for j in range(PAIR):
+                    xt = xt_psum.tile([P, PASSES, 2, P], F32, name="xt")
+                    for g in range(PASSES):
+                        for u in range(2):
+                            first = g * (K // PASSES // 2) + u
+                            nc.tensor.transpose(
+                                xt[:, g, u, :],
+                                words[:, half * PAIR + j, first : first + 2 * P - 1 : 2],
+                                ident[:],
+                            )
+                    nc.scalar.copy(
+                        out=grouped[:, j].bitcast(F32),
+                        in_=xt[:].rearrange("p g u r -> p g r u"),
+                    )
+                mx_tiles[(r, half)] = [grouped]
+
+        def quantise_round(r):
+            for half in range(ROUND // PAIR):
+                grouped = mx_tiles[(r, half)][0]
+                codes = mx_pool.tile([P, PAIR, PASSES, P], U32, align_bytes=64, name="codes")
+                scales = mx_pool.tile([P, PAIR, PASSES, P], U8, align_bytes=64, name="scales")
+                nc.vector.quantize_mx(
+                    out=codes[:].rearrange("p j g r -> p (j g r)").bitcast(FP8X4),
+                    scales=scales[:].rearrange("p j g r -> p (j g r)"),
+                    in_=grouped[:].rearrange("p j g r t -> p (j g r t)"),
+                )
+                mx_tiles[(r, half)] = [codes, scales]
+
+        def make_tables(r):
+            t0 = r * ROUND
+            cos_twice = table_pool.tile([P, ROUND, D], BF16, name="cos_twice")
+            minus_sin = table_pool.tile([P, ROUND, HALF_D], BF16, name="minus_sin")
+            nc.scalar.copy(
+                out=cos_twice[:].rearrange("p t (i h) -> p t i h", h=2),
+                in_=rope_pairs[:, t0 : t0 + ROUND, :, 0:1].to_broadcast([P, ROUND, HALF_D, 2]),
+            )
+            nc.scalar.mul(out=minus_sin[:], in_=rope_pairs[:, t0 : t0 + ROUND, :, 1], mul=-1.0)
+            table_tiles[r] = [cos_twice, minus_sin]
+
+        def multiply_round(r):
+            v_acc = v_psum.tile([P, ROUND, HEADS, D], F32, name="v_acc")
+            qk_accs = []
+            for half in range(ROUND // PAIR):
+                codes, scales = mx_tiles[(r, half)]
+                qk_acc = qk_psum.tile([P, PAIR, 2 * HEADS, D], F32, name="qk_acc")
+                qk_accs.append(qk_acc)
+                for j in range(PAIR):
+                    targets = [
+                        qk_acc[:, j, 0:HEADS, :],
+                        qk_acc[:, j, HEADS : 2 * HEADS, :],
+                        v_acc[:, half * PAIR + j, :, :],
+                    ]
+                    for c in range(3):
+                        for g in range(PASSES):
+                            nc.tensor.matmul_mx(
+                                out=targets[c].rearrange("p h d -> p (h d)"),
+                                lhsT=codes[:, j, g, :].bitcast(FP8X4),
+                                lhsT_scale=scales[:, j, g, :],
+                                rhs=w_code_sb[:, g, 2 * BLOCK * c : 2 * BLOCK * (c + 1)].bitcast(
+                                    FP4X4
+                                ),
+                                rhs_scale=w_scale_sb[:, g, BLOCK * c : BLOCK * (c + 1)],
+                                start=(g == 0),
+                                stop=(g == PASSES - 1),
+                            )
+            res_tiles[r] = [qk_accs, v_acc]
+
+        def rotate_round(r):
+            t0 = r * ROUND
+            qk_accs, v_acc = res_tiles[r]
+            cos_twice, minus_sin = table_tiles[r]
+            res_qk = res_pool.tile([P, 2 * HEADS, ROUND, D], F32, name="res_qk")
+            res_v = res_pool.tile([P, HEADS, ROUND, D], F32, name="res_v")
+            cross = res_pool.tile([P, 2, 2 * HEADS, ROUND, HALF_D], F32, name="cross")
+            for half in range(ROUND // PAIR):
+                tiles = slice(half * PAIR, (half + 1) * PAIR)
+                acc = qk_accs[half]
+                acc_pairs = acc[:].rearrange("p t c (i h) -> p t c i h", h=2)
+                nc.vector.tensor_tensor(
+                    out=res_qk[:, :, tiles, :].rearrange("p c t d -> p t c d"),
+                    in0=acc[:],
+                    in1=cos_twice[:, tiles, :].unsqueeze(2).to_broadcast([P, PAIR, 2 * HEADS, D]),
+                    op=MULT,
+                )
+                nc.vector.tensor_tensor(
+                    out=cross[:, 0, :, tiles, :].rearrange("p c t i -> p t c i"),
+                    in0=acc_pairs[:, :, :, :, 1],
+                    in1=minus_sin[:, tiles, :]
+                    .unsqueeze(2)
+                    .to_broadcast([P, PAIR, 2 * HEADS, HALF_D]),
+                    op=MULT,
+                )
+                nc.vector.tensor_tensor(
+                    out=cross[:, 1, :, tiles, :].rearrange("p c t i -> p t c i"),
+                    in0=acc_pairs[:, :, :, :, 0],
+                    in1=rope_pairs[:, t0 + half * PAIR : t0 + (half + 1) * PAIR, :, 1]
+                    .unsqueeze(2)
+                    .to_broadcast([P, PAIR, 2 * HEADS, HALF_D]),
+                    op=MULT,
+                )
+            nc.scalar.copy(out=res_v[:].rearrange("p h t d -> p t h d"), in_=v_acc[:])
+            res_pairs = res_qk[:].rearrange("p c t (i h) -> p (c t i) h", h=2)
+            nc.gpsimd.tensor_tensor(
+                out=res_pairs,
+                in0=res_pairs,
+                in1=cross[:].rearrange("p h c t i -> p (c t i) h"),
+                op=ADD,
+            )
+            res_tiles[r] = [res_qk, res_v]
+
+        def store_round(r):
+            tiles = slice(r * ROUND, (r + 1) * ROUND)
+            res_qk, res_v = res_tiles[r]
+            nc.sync.dma_start(out=out_v_v[:, :, tiles, :], in_=res_v[:])
+            nc.sync.dma_start(out=out_q_v[:, :, tiles, :], in_=res_qk[:, 0:HEADS, :, :])
+            nc.sync.dma_start(out=out_k_v[:, :, tiles, :], in_=res_qk[:, HEADS : 2 * HEADS, :, :])
+
+        for i in range(ROUNDS + 2):
+            if i + LOAD_AHEAD < ROUNDS:
+                load_round(i + LOAD_AHEAD, 1)
+            if i < ROUNDS:
+                transpose_round(i)
+                make_tables(i)
+            if 1 <= i <= ROUNDS:
+                multiply_round(i - 1)
+            if i < ROUNDS:
+                quantise_round(i)
+            if 1 <= i <= ROUNDS:
+                rotate_round(i - 1)
+            if i >= 2:
+                store_round(i - 2)

@@ -202,7 +202,7 @@ def tile_jointattention_pa_t_kernel(
                 )
             nc.scalar.copy(out=res_v[:].rearrange("p h t d -> p t h d"), in_=v_acc[:])
             res_pairs = res_qk[:].rearrange("p c t (i h) -> p (c t i) h", h=2)
-            nc.gpsimd.tensor_tensor(
+            nc.vector.tensor_tensor(
                 out=res_pairs,
                 in0=res_pairs,
                 in1=cross[:].rearrange("p h c t i -> p (c t i) h"),

@@ -131,13 +131,17 @@ def tile_jointattention_pa_t_kernel(
         def make_tables(r):
             t0 = r * ROUND
             cos_twice = table_pool.tile([P, ROUND, D], BF16, name="cos_twice")
-            minus_sin = table_pool.tile([P, ROUND, HALF_D], BF16, name="minus_sin")
+            signed_sin = table_pool.tile([P, ROUND, D], BF16, name="signed_sin")
+            sin_pairs = signed_sin[:].rearrange("p t (i h) -> p t i h", h=2)
             nc.scalar.copy(
                 out=cos_twice[:].rearrange("p t (i h) -> p t i h", h=2),
                 in_=rope_pairs[:, t0 : t0 + ROUND, :, 0:1].to_broadcast([P, ROUND, HALF_D, 2]),
             )
-            nc.scalar.mul(out=minus_sin[:], in_=rope_pairs[:, t0 : t0 + ROUND, :, 1], mul=-1.0)
-            table_tiles[r] = [cos_twice, minus_sin]
+            nc.scalar.mul(
+                out=sin_pairs[:, :, :, 0], in_=rope_pairs[:, t0 : t0 + ROUND, :, 1], mul=-1.0
+            )
+            nc.scalar.copy(out=sin_pairs[:, :, :, 1], in_=rope_pairs[:, t0 : t0 + ROUND, :, 1])
+            table_tiles[r] = [cos_twice, signed_sin]
 
         def multiply_round(r):
             v_acc = v_psum.tile([P, ROUND, HEADS, D], F32, name="v_acc")
@@ -168,46 +172,42 @@ def tile_jointattention_pa_t_kernel(
             res_tiles[r] = [qk_accs, v_acc]
 
         def rotate_round(r):
-            t0 = r * ROUND
             qk_accs, v_acc = res_tiles[r]
-            cos_twice, minus_sin = table_tiles[r]
+            cos_twice, signed_sin = table_tiles[r]
             res_qk = res_pool.tile([P, 2 * HEADS, ROUND, D], F32, name="res_qk")
             res_v = res_pool.tile([P, HEADS, ROUND, D], F32, name="res_v")
-            cross = res_pool.tile([P, 2, 2 * HEADS, ROUND, HALF_D], F32, name="cross")
+            cross = res_pool.tile([P, 2 * HEADS, ROUND, D], F32, name="cross")
+            shape = [P, PAIR, 2 * HEADS, HALF_D, 2]
             for half in range(ROUND // PAIR):
                 tiles = slice(half * PAIR, (half + 1) * PAIR)
-                acc = qk_accs[half]
-                acc_pairs = acc[:].rearrange("p t c (i h) -> p t c i h", h=2)
+                acc_pairs = qk_accs[half][:].rearrange("p t c (i h) -> p t c i h", h=2)
                 nc.vector.tensor_tensor(
-                    out=res_qk[:, :, tiles, :].rearrange("p c t d -> p t c d"),
-                    in0=acc[:],
-                    in1=cos_twice[:, tiles, :].unsqueeze(2).to_broadcast([P, PAIR, 2 * HEADS, D]),
+                    out=res_qk[:, :, tiles, :].rearrange("p c t (i h) -> p t c i h", h=2),
+                    in0=acc_pairs,
+                    in1=cos_twice[:, tiles, :]
+                    .rearrange("p t (i h) -> p t i h", h=2)
+                    .unsqueeze(2)
+                    .to_broadcast(shape),
                     op=MULT,
                 )
                 nc.vector.tensor_tensor(
-                    out=cross[:, 0, :, tiles, :].rearrange("p c t i -> p t c i"),
-                    in0=acc_pairs[:, :, :, :, 1],
-                    in1=minus_sin[:, tiles, :]
+                    out=cross[:, :, tiles, :].rearrange("p c t (i h) -> p t c i h", h=2),
+                    in0=acc_pairs[:, :, :, :, ::-1],
+                    in1=signed_sin[:, tiles, :]
+                    .rearrange("p t (i h) -> p t i h", h=2)
                     .unsqueeze(2)
-                    .to_broadcast([P, PAIR, 2 * HEADS, HALF_D]),
-                    op=MULT,
-                )
-                nc.vector.tensor_tensor(
-                    out=cross[:, 1, :, tiles, :].rearrange("p c t i -> p t c i"),
-                    in0=acc_pairs[:, :, :, :, 0],
-                    in1=rope_pairs[:, t0 + half * PAIR : t0 + (half + 1) * PAIR, :, 1]
-                    .unsqueeze(2)
-                    .to_broadcast([P, PAIR, 2 * HEADS, HALF_D]),
+                    .to_broadcast(shape),
                     op=MULT,
                 )
             nc.scalar.copy(out=res_v[:].rearrange("p h t d -> p t h d"), in_=v_acc[:])
-            res_pairs = res_qk[:].rearrange("p c t (i h) -> p (c t i) h", h=2)
-            nc.vector.tensor_tensor(
-                out=res_pairs,
-                in0=res_pairs,
-                in1=cross[:].rearrange("p h c t i -> p (c t i) h"),
-                op=ADD,
-            )
+            for half in range(ROUND // PAIR):
+                tiles = slice(half * PAIR, (half + 1) * PAIR)
+                nc.vector.tensor_tensor(
+                    out=res_qk[:, :, tiles, :],
+                    in0=res_qk[:, :, tiles, :],
+                    in1=cross[:, :, tiles, :],
+                    op=ADD,
+                )
             res_tiles[r] = [res_qk, res_v]
 
         def store_round(r):

@@ -116,17 +116,16 @@ def tile_jointattention_pa_t_kernel(
                     )
                 mx_tiles[(r, half)] = [grouped]
 
-        def quantise_round(r):
-            for half in range(ROUND // PAIR):
-                grouped = mx_tiles[(r, half)][0]
-                codes = mx_pool.tile([P, PAIR, PASSES, P], U32, align_bytes=64, name="codes")
-                scales = mx_pool.tile([P, PAIR, PASSES, P], U8, align_bytes=64, name="scales")
-                nc.vector.quantize_mx(
-                    out=codes[:].rearrange("p j g r -> p (j g r)").bitcast(FP8X4),
-                    scales=scales[:].rearrange("p j g r -> p (j g r)"),
-                    in_=grouped[:].rearrange("p j g r t -> p (j g r t)"),
-                )
-                mx_tiles[(r, half)] = [codes, scales]
+        def quantise_half(r, half):
+            grouped = mx_tiles[(r, half)][0]
+            codes = mx_pool.tile([P, PAIR, PASSES, P], U32, align_bytes=64, name="codes")
+            scales = mx_pool.tile([P, PAIR, PASSES, P], U8, align_bytes=64, name="scales")
+            nc.vector.quantize_mx(
+                out=codes[:].rearrange("p j g r -> p (j g r)").bitcast(FP8X4),
+                scales=scales[:].rearrange("p j g r -> p (j g r)"),
+                in_=grouped[:].rearrange("p j g r t -> p (j g r t)"),
+            )
+            mx_tiles[(r, half)] = [codes, scales]
 
         def make_tables(r):
             t0 = r * ROUND
@@ -171,48 +170,48 @@ def tile_jointattention_pa_t_kernel(
                             )
             res_tiles[r] = [qk_accs, v_acc]
 
-        def rotate_round(r):
+        def open_results(r):
             qk_accs, v_acc = res_tiles[r]
-            cos_twice, signed_sin = table_tiles[r]
             res_qk = res_pool.tile([P, 2 * HEADS, ROUND, D], F32, name="res_qk")
             res_v = res_pool.tile([P, HEADS, ROUND, D], F32, name="res_v")
             cross = res_pool.tile([P, 2 * HEADS, ROUND, D], F32, name="cross")
-            shape = [P, PAIR, 2 * HEADS, HALF_D, 2]
-            for half in range(ROUND // PAIR):
-                tiles = slice(half * PAIR, (half + 1) * PAIR)
-                acc_pairs = qk_accs[half][:].rearrange("p t c (i h) -> p t c i h", h=2)
-                nc.vector.tensor_tensor(
-                    out=res_qk[:, :, tiles, :].rearrange("p c t (i h) -> p t c i h", h=2),
-                    in0=acc_pairs,
-                    in1=cos_twice[:, tiles, :]
-                    .rearrange("p t (i h) -> p t i h", h=2)
-                    .unsqueeze(2)
-                    .to_broadcast(shape),
-                    op=MULT,
-                )
-                nc.vector.tensor_tensor(
-                    out=cross[:, :, tiles, :].rearrange("p c t (i h) -> p t c i h", h=2),
-                    in0=acc_pairs[:, :, :, :, ::-1],
-                    in1=signed_sin[:, tiles, :]
-                    .rearrange("p t (i h) -> p t i h", h=2)
-                    .unsqueeze(2)
-                    .to_broadcast(shape),
-                    op=MULT,
-                )
             nc.scalar.copy(out=res_v[:].rearrange("p h t d -> p t h d"), in_=v_acc[:])
-            for half in range(ROUND // PAIR):
-                tiles = slice(half * PAIR, (half + 1) * PAIR)
-                nc.vector.tensor_tensor(
-                    out=res_qk[:, :, tiles, :],
-                    in0=res_qk[:, :, tiles, :],
-                    in1=cross[:, :, tiles, :],
-                    op=ADD,
-                )
-            res_tiles[r] = [res_qk, res_v]
+            res_tiles[r] = [qk_accs, res_qk, res_v, cross]
+
+        def rotate_half(r, half):
+            qk_accs, res_qk, res_v, cross = res_tiles[r]
+            cos_twice, signed_sin = table_tiles[r]
+            shape = [P, PAIR, 2 * HEADS, HALF_D, 2]
+            tiles = slice(half * PAIR, (half + 1) * PAIR)
+            acc_pairs = qk_accs[half][:].rearrange("p t c (i h) -> p t c i h", h=2)
+            nc.vector.tensor_tensor(
+                out=res_qk[:, :, tiles, :].rearrange("p c t (i h) -> p t c i h", h=2),
+                in0=acc_pairs,
+                in1=cos_twice[:, tiles, :]
+                .rearrange("p t (i h) -> p t i h", h=2)
+                .unsqueeze(2)
+                .to_broadcast(shape),
+                op=MULT,
+            )
+            nc.vector.tensor_tensor(
+                out=cross[:, :, tiles, :].rearrange("p c t (i h) -> p t c i h", h=2),
+                in0=acc_pairs[:, :, :, :, ::-1],
+                in1=signed_sin[:, tiles, :]
+                .rearrange("p t (i h) -> p t i h", h=2)
+                .unsqueeze(2)
+                .to_broadcast(shape),
+                op=MULT,
+            )
+            nc.gpsimd.tensor_tensor(
+                out=res_qk[:, :, tiles, :],
+                in0=res_qk[:, :, tiles, :],
+                in1=cross[:, :, tiles, :],
+                op=ADD,
+            )
 
         def store_round(r):
             tiles = slice(r * ROUND, (r + 1) * ROUND)
-            res_qk, res_v = res_tiles[r]
+            res_qk, res_v = res_tiles[r][1:3]
             nc.sync.dma_start(out=out_v_v[:, :, tiles, :], in_=res_v[:])
             nc.sync.dma_start(out=out_q_v[:, :, tiles, :], in_=res_qk[:, 0:HEADS, :, :])
             nc.sync.dma_start(out=out_k_v[:, :, tiles, :], in_=res_qk[:, HEADS : 2 * HEADS, :, :])
@@ -225,9 +224,11 @@ def tile_jointattention_pa_t_kernel(
                 make_tables(i)
             if 1 <= i <= ROUNDS:
                 multiply_round(i - 1)
-            if i < ROUNDS:
-                quantise_round(i)
-            if 1 <= i <= ROUNDS:
-                rotate_round(i - 1)
+                open_results(i - 1)
+            for half in range(ROUND // PAIR):
+                if i < ROUNDS:
+                    quantise_half(i, half)
+                if 1 <= i <= ROUNDS:
+                    rotate_half(i - 1, half)
             if i >= 2:
                 store_round(i - 2)

@@ -94,27 +94,26 @@ def tile_jointattention_pa_t_kernel(
         for r in range(1, LOAD_AHEAD):
             load_round(r, 1)
 
-        def transpose_round(r):
+        def transpose_half(r, half):
             words = x_tiles[r][:].bitcast(F32)
-            for half in range(ROUND // PAIR):
-                grouped = mx_pool.tile(
-                    [P, PAIR, PASSES, P, PACK], BF16, align_bytes=64, name="grouped"
+            grouped = mx_pool.tile(
+                [P, PAIR, PASSES, P, PACK], BF16, align_bytes=64, name="grouped"
+            )
+            for j in range(PAIR):
+                xt = xt_psum.tile([P, PASSES, 2, P], F32, name="xt")
+                for g in range(PASSES):
+                    for u in range(2):
+                        first = g * (K // PASSES // 2) + u
+                        nc.tensor.transpose(
+                            xt[:, g, u, :],
+                            words[:, half * PAIR + j, first : first + 2 * P - 1 : 2],
+                            ident[:],
+                        )
+                nc.scalar.copy(
+                    out=grouped[:, j].bitcast(F32),
+                    in_=xt[:].rearrange("p g u r -> p g r u"),
                 )
-                for j in range(PAIR):
-                    xt = xt_psum.tile([P, PASSES, 2, P], F32, name="xt")
-                    for g in range(PASSES):
-                        for u in range(2):
-                            first = g * (K // PASSES // 2) + u
-                            nc.tensor.transpose(
-                                xt[:, g, u, :],
-                                words[:, half * PAIR + j, first : first + 2 * P - 1 : 2],
-                                ident[:],
-                            )
-                    nc.scalar.copy(
-                        out=grouped[:, j].bitcast(F32),
-                        in_=xt[:].rearrange("p g u r -> p g r u"),
-                    )
-                mx_tiles[(r, half)] = [grouped]
+            mx_tiles[(r, half)] = [grouped]
 
         def quantise_half(r, half):
             grouped = mx_tiles[(r, half)][0]
@@ -142,33 +141,31 @@ def tile_jointattention_pa_t_kernel(
             nc.scalar.copy(out=sin_pairs[:, :, :, 1], in_=rope_pairs[:, t0 : t0 + ROUND, :, 1])
             table_tiles[r] = [cos_twice, signed_sin]
 
-        def multiply_round(r):
-            v_acc = v_psum.tile([P, ROUND, HEADS, D], F32, name="v_acc")
-            qk_accs = []
-            for half in range(ROUND // PAIR):
-                codes, scales = mx_tiles[(r, half)]
-                qk_acc = qk_psum.tile([P, PAIR, 2 * HEADS, D], F32, name="qk_acc")
-                qk_accs.append(qk_acc)
-                for j in range(PAIR):
-                    targets = [
-                        qk_acc[:, j, 0:HEADS, :],
-                        qk_acc[:, j, HEADS : 2 * HEADS, :],
-                        v_acc[:, half * PAIR + j, :, :],
-                    ]
-                    for c in range(3):
-                        for g in range(PASSES):
-                            nc.tensor.matmul_mx(
-                                out=targets[c].rearrange("p h d -> p (h d)"),
-                                lhsT=codes[:, j, g, :].bitcast(FP8X4),
-                                lhsT_scale=scales[:, j, g, :],
-                                rhs=w_code_sb[:, g, 2 * BLOCK * c : 2 * BLOCK * (c + 1)].bitcast(
-                                    FP4X4
-                                ),
-                                rhs_scale=w_scale_sb[:, g, BLOCK * c : BLOCK * (c + 1)],
-                                start=(g == 0),
-                                stop=(g == PASSES - 1),
-                            )
-            res_tiles[r] = [qk_accs, v_acc]
+        def multiply_half(r, half):
+            if half == 0:
+                v_acc = v_psum.tile([P, ROUND, HEADS, D], F32, name="v_acc")
+                res_tiles[r] = [[], v_acc]
+            qk_accs, v_acc = res_tiles[r]
+            codes, scales = mx_tiles[(r, half)]
+            qk_acc = qk_psum.tile([P, PAIR, 2 * HEADS, D], F32, name="qk_acc")
+            qk_accs.append(qk_acc)
+            for j in range(PAIR):
+                targets = [
+                    qk_acc[:, j, 0:HEADS, :],
+                    qk_acc[:, j, HEADS : 2 * HEADS, :],
+                    v_acc[:, half * PAIR + j, :, :],
+                ]
+                for c in range(3):
+                    for g in range(PASSES):
+                        nc.tensor.matmul_mx(
+                            out=targets[c].rearrange("p h d -> p (h d)"),
+                            lhsT=codes[:, j, g, :].bitcast(FP8X4),
+                            lhsT_scale=scales[:, j, g, :],
+                            rhs=w_code_sb[:, g, 2 * BLOCK * c : 2 * BLOCK * (c + 1)].bitcast(FP4X4),
+                            rhs_scale=w_scale_sb[:, g, BLOCK * c : BLOCK * (c + 1)],
+                            start=(g == 0),
+                            stop=(g == PASSES - 1),
+                        )
 
         def open_results(r):
             qk_accs, v_acc = res_tiles[r]
@@ -219,11 +216,14 @@ def tile_jointattention_pa_t_kernel(
         for i in range(ROUNDS + 2):
             if i + LOAD_AHEAD < ROUNDS:
                 load_round(i + LOAD_AHEAD, 1)
+            for half in range(ROUND // PAIR):
+                if i < ROUNDS:
+                    transpose_half(i, half)
+                if 1 <= i <= ROUNDS:
+                    multiply_half(i - 1, half)
             if i < ROUNDS:
-                transpose_round(i)
                 make_tables(i)
             if 1 <= i <= ROUNDS:
-                multiply_round(i - 1)
                 open_results(i - 1)
             for half in range(ROUND // PAIR):
                 if i < ROUNDS:

@@ -28,6 +28,7 @@ PAIR = 2
 ROUND = 4
 ROUNDS = TILES // ROUND
 LOAD_AHEAD = 4
+ROPE_ROUNDS = 4
 
 FLOPS = 2 * TOKENS * K * COLS
 
@@ -88,11 +89,20 @@ def tile_jointattention_pa_t_kernel(
                 .rearrange("g r n -> r g n")
                 .bitcast(I32),
             )
-        rope_sb = const.tile([P, TILES, D], BF16)
-        nc.sync.dma_start(out=rope_sb[:], in_=rope_v)
-        rope_pairs = rope_sb[:].rearrange("p t (i h) -> p t i h", h=2)
-        for r in range(1, LOAD_AHEAD):
+        rope_parts = []
+
+        def load_rope_part():
+            first = len(rope_parts) * ROPE_ROUNDS * ROUND
+            rope_sb = const.tile([P, ROPE_ROUNDS * ROUND, D], BF16, name="rope%d" % len(rope_parts))
+            nc.sync.dma_start(out=rope_sb[:], in_=rope_v[:, first : first + ROPE_ROUNDS * ROUND, :])
+            rope_parts.append(rope_sb)
+
+        load_round(1, 1)
+        load_rope_part()
+        for r in range(2, LOAD_AHEAD):
             load_round(r, 1)
+        for part in range(1, ROUNDS // ROPE_ROUNDS):
+            load_rope_part()
 
         def transpose_half(r, half):
             words = x_tiles[r][:].bitcast(F32)
@@ -127,7 +137,10 @@ def tile_jointattention_pa_t_kernel(
             mx_tiles[(r, half)] = [codes, scales]
 
         def make_tables(r):
-            t0 = r * ROUND
+            t0 = (r % ROPE_ROUNDS) * ROUND
+            rope_pairs = rope_parts[r // ROPE_ROUNDS][:].rearrange(
+                "p t (i h) -> p t i h", h=2
+            )
             cos_twice = table_pool.tile([P, ROUND, D], BF16, name="cos_twice")
             signed_sin = table_pool.tile([P, ROUND, D], BF16, name="signed_sin")
             sin_pairs = signed_sin[:].rearrange("p t (i h) -> p t i h", h=2)
@@ -149,23 +162,19 @@ def tile_jointattention_pa_t_kernel(
             codes, scales = mx_tiles[(r, half)]
             qk_acc = qk_psum.tile([P, PAIR, 2 * HEADS, D], F32, name="qk_acc")
             qk_accs.append(qk_acc)
-            for j in range(PAIR):
-                targets = [
-                    qk_acc[:, j, 0:HEADS, :],
-                    qk_acc[:, j, HEADS : 2 * HEADS, :],
-                    v_acc[:, half * PAIR + j, :, :],
-                ]
-                for c in range(3):
-                    for g in range(PASSES):
-                        nc.tensor.matmul_mx(
-                            out=targets[c].rearrange("p h d -> p (h d)"),
-                            lhsT=codes[:, j, g, :].bitcast(FP8X4),
-                            lhsT_scale=scales[:, j, g, :],
-                            rhs=w_code_sb[:, g, 2 * BLOCK * c : 2 * BLOCK * (c + 1)].bitcast(FP4X4),
-                            rhs_scale=w_scale_sb[:, g, BLOCK * c : BLOCK * (c + 1)],
-                            start=(g == 0),
-                            stop=(g == PASSES - 1),
-                        )
+            products = [(j, c, qk_acc[:, j, HEADS * c : HEADS * (c + 1), :]) for j in range(PAIR) for c in range(2)]
+            products.extend([(j, 2, v_acc[:, half * PAIR + j, :, :]) for j in range(PAIR)])
+            for j, c, target in products:
+                for g in range(PASSES):
+                    nc.tensor.matmul_mx(
+                        out=target.rearrange("p h d -> p (h d)"),
+                        lhsT=codes[:, j, g, :].bitcast(FP8X4),
+                        lhsT_scale=scales[:, j, g, :],
+                        rhs=w_code_sb[:, g, 2 * BLOCK * c : 2 * BLOCK * (c + 1)].bitcast(FP4X4),
+                        rhs_scale=w_scale_sb[:, g, BLOCK * c : BLOCK * (c + 1)],
+                        start=(g == 0),
+                        stop=(g == PASSES - 1),
+                    )
 
         def open_results(r):
             qk_accs, v_acc = res_tiles[r]
@@ -199,21 +208,28 @@ def tile_jointattention_pa_t_kernel(
                 .to_broadcast(shape),
                 op=MULT,
             )
-            nc.gpsimd.tensor_tensor(
+            adder = nc.vector if (r, half) == (ROUNDS - 1, ROUND // PAIR - 1) else nc.gpsimd
+            adder.tensor_tensor(
                 out=res_qk[:, :, tiles, :],
                 in0=res_qk[:, :, tiles, :],
                 in1=cross[:, :, tiles, :],
                 op=ADD,
             )
 
-        def store_round(r):
+        def store_v(r):
             tiles = slice(r * ROUND, (r + 1) * ROUND)
-            res_qk, res_v = res_tiles[r][1:3]
-            nc.sync.dma_start(out=out_v_v[:, :, tiles, :], in_=res_v[:])
-            nc.sync.dma_start(out=out_q_v[:, :, tiles, :], in_=res_qk[:, 0:HEADS, :, :])
-            nc.sync.dma_start(out=out_k_v[:, :, tiles, :], in_=res_qk[:, HEADS : 2 * HEADS, :, :])
+            nc.sync.dma_start(out=out_v_v[:, :, tiles, :], in_=res_tiles[r][2][:])
 
-        for i in range(ROUNDS + 2):
+        def store_qk(r, first, count):
+            tiles = slice(r * ROUND + first, r * ROUND + first + count)
+            kept = slice(first, first + count)
+            res_qk = res_tiles[r][1]
+            nc.sync.dma_start(out=out_q_v[:, :, tiles, :], in_=res_qk[:, 0:HEADS, kept, :])
+            nc.sync.dma_start(
+                out=out_k_v[:, :, tiles, :], in_=res_qk[:, HEADS : 2 * HEADS, kept, :]
+            )
+
+        for i in range(ROUNDS + 1):
             if i + LOAD_AHEAD < ROUNDS:
                 load_round(i + LOAD_AHEAD, 1)
             for half in range(ROUND // PAIR):
@@ -225,10 +241,17 @@ def tile_jointattention_pa_t_kernel(
                 make_tables(i)
             if 1 <= i <= ROUNDS:
                 open_results(i - 1)
+            if i == ROUNDS:
+                store_v(i - 2)
+                store_qk(i - 2, 0, ROUND)
+                store_v(i - 1)
             for half in range(ROUND // PAIR):
                 if i < ROUNDS:
                     quantise_half(i, half)
                 if 1 <= i <= ROUNDS:
                     rotate_half(i - 1, half)
-            if i >= 2:
-                store_round(i - 2)
+                if i == ROUNDS:
+                    store_qk(i - 1, half * PAIR, PAIR)
+            if 2 <= i < ROUNDS:
+                store_v(i - 2)
+                store_qk(i - 2, 0, ROUND)

@@ -29,6 +29,8 @@ ROUND = 4
 ROUNDS = TILES // ROUND
 LOAD_AHEAD = 4
 ROPE_ROUNDS = 4
+GPSIMD_BLOCKS = 3
+LAST_HALF = (ROUNDS - 1, ROUND // PAIR - 1)
 
 FLOPS = 2 * TOKENS * K * COLS
 
@@ -208,11 +210,17 @@ def tile_jointattention_pa_t_kernel(
                 .to_broadcast(shape),
                 op=MULT,
             )
-            adder = nc.vector if (r, half) == (ROUNDS - 1, ROUND // PAIR - 1) else nc.gpsimd
-            adder.tensor_tensor(
-                out=res_qk[:, :, tiles, :],
-                in0=res_qk[:, :, tiles, :],
-                in1=cross[:, :, tiles, :],
+            if (r, half) != LAST_HALF:
+                add_products(nc.gpsimd, r, half, 0, GPSIMD_BLOCKS)
+
+        def add_products(engine, r, half, first, count):
+            res_qk, cross = res_tiles[r][1], res_tiles[r][3]
+            tiles = slice(half * PAIR, (half + 1) * PAIR)
+            blocks = slice(first, first + count)
+            engine.tensor_tensor(
+                out=res_qk[:, blocks, tiles, :],
+                in0=res_qk[:, blocks, tiles, :],
+                in1=cross[:, blocks, tiles, :],
                 op=ADD,
             )
 
@@ -235,23 +243,31 @@ def tile_jointattention_pa_t_kernel(
             for half in range(ROUND // PAIR):
                 if i < ROUNDS:
                     transpose_half(i, half)
+            for half in range(ROUND // PAIR):
                 if 1 <= i <= ROUNDS:
                     multiply_half(i - 1, half)
             if i < ROUNDS:
                 make_tables(i)
             if 1 <= i <= ROUNDS:
                 open_results(i - 1)
-            if i == ROUNDS:
-                store_v(i - 2)
-                store_qk(i - 2, 0, ROUND)
-                store_v(i - 1)
             for half in range(ROUND // PAIR):
                 if i < ROUNDS:
                     quantise_half(i, half)
                 if 1 <= i <= ROUNDS:
                     rotate_half(i - 1, half)
-                if i == ROUNDS:
-                    store_qk(i - 1, half * PAIR, PAIR)
+                    before = (i - 1, 0) if half == 1 else (i - 2, 1)
+                    if before[0] >= 0:
+                        add_products(
+                            nc.vector, before[0], before[1], GPSIMD_BLOCKS, 2 * HEADS - GPSIMD_BLOCKS
+                        )
+                if i == ROUNDS and half == 0:
+                    store_v(i - 2)
+                    store_qk(i - 2, 0, ROUND)
+                    store_v(i - 1)
+            if i == ROUNDS:
+                store_qk(i - 1, 0, PAIR)
+                add_products(nc.vector, i - 1, 1, 0, 2 * HEADS)
+                store_qk(i - 1, PAIR, PAIR)
             if 2 <= i < ROUNDS:
                 store_v(i - 2)
                 store_qk(i - 2, 0, ROUND)

@@ -29,6 +29,8 @@ ROUND = 4
 ROUNDS = TILES // ROUND
 LOAD_AHEAD = 4
 ROPE_ROUNDS = 4
+WARM_FIRST = 5
+WARM_BETWEEN = 2
 GPSIMD_BLOCKS = 3
 LAST_HALF = (ROUNDS - 1, ROUND // PAIR - 1)
 
@@ -72,12 +74,23 @@ def tile_jointattention_pa_t_kernel(
                 )
             x_tiles[r] = x_sb
 
+        idle_sb = const.tile([P, 4 * P], BF16)
+        nc.vector.memset(idle_sb[:], 0.0)
         w_scale_sb = const.tile([P, PASSES, COLS], U8, align_bytes=64)
         nc.vector.memset(w_scale_sb[:].bitcast(I32), 0)
         ident = const.tile([P, P], F32)
         make_identity(nc, ident[:])
 
         load_round(0, ROUND)
+
+        def keep_busy(count):
+            idle_acc = v_psum.tile([P, 4 * P], F32, name="v_acc")
+            for n in range(count):
+                nc.tensor.matmul(
+                    idle_acc[:], lhsT=idle_sb[:, 0:P], rhs=idle_sb[:], start=True, stop=True
+                )
+
+        keep_busy(WARM_FIRST)
 
         w_code_sb = const.tile([P, PASSES, 2 * COLS], U8, align_bytes=64)
         nc.sync.dma_start(
@@ -143,18 +156,13 @@ def tile_jointattention_pa_t_kernel(
             rope_pairs = rope_parts[r // ROPE_ROUNDS][:].rearrange(
                 "p t (i h) -> p t i h", h=2
             )
-            cos_twice = table_pool.tile([P, ROUND, D], BF16, name="cos_twice")
             signed_sin = table_pool.tile([P, ROUND, D], BF16, name="signed_sin")
             sin_pairs = signed_sin[:].rearrange("p t (i h) -> p t i h", h=2)
-            nc.scalar.copy(
-                out=cos_twice[:].rearrange("p t (i h) -> p t i h", h=2),
-                in_=rope_pairs[:, t0 : t0 + ROUND, :, 0:1].to_broadcast([P, ROUND, HALF_D, 2]),
-            )
             nc.scalar.mul(
                 out=sin_pairs[:, :, :, 0], in_=rope_pairs[:, t0 : t0 + ROUND, :, 1], mul=-1.0
             )
             nc.scalar.copy(out=sin_pairs[:, :, :, 1], in_=rope_pairs[:, t0 : t0 + ROUND, :, 1])
-            table_tiles[r] = [cos_twice, signed_sin]
+            table_tiles[r] = signed_sin
 
         def multiply_half(r, half):
             if half == 0:
@@ -188,17 +196,18 @@ def tile_jointattention_pa_t_kernel(
 
         def rotate_half(r, half):
             qk_accs, res_qk, res_v, cross = res_tiles[r]
-            cos_twice, signed_sin = table_tiles[r]
+            signed_sin = table_tiles[r]
             shape = [P, PAIR, 2 * HEADS, HALF_D, 2]
             tiles = slice(half * PAIR, (half + 1) * PAIR)
+            listed = (r % ROPE_ROUNDS) * ROUND + half * PAIR
             acc_pairs = qk_accs[half][:].rearrange("p t c (i h) -> p t c i h", h=2)
             nc.vector.tensor_tensor(
-                out=res_qk[:, :, tiles, :].rearrange("p c t (i h) -> p t c i h", h=2),
-                in0=acc_pairs,
-                in1=cos_twice[:, tiles, :]
-                .rearrange("p t (i h) -> p t i h", h=2)
-                .unsqueeze(2)
-                .to_broadcast(shape),
+                out=res_qk[:, :, tiles, :].rearrange("p c t (i h) -> p c t i h", h=2),
+                in0=acc_pairs.rearrange("p t c i h -> p c t i h"),
+                in1=rope_parts[r // ROPE_ROUNDS][:, listed : listed + PAIR, :]
+                .rearrange("p t (i h) -> p t i h", h=2)[:, :, :, 0:1]
+                .unsqueeze(1)
+                .to_broadcast([P, 2 * HEADS, PAIR, HALF_D, 2]),
                 op=MULT,
             )
             nc.vector.tensor_tensor(
@@ -243,6 +252,8 @@ def tile_jointattention_pa_t_kernel(
             for half in range(ROUND // PAIR):
                 if i < ROUNDS:
                     transpose_half(i, half)
+            if i == 0:
+                keep_busy(WARM_BETWEEN)
             for half in range(ROUND // PAIR):
                 if 1 <= i <= ROUNDS:
                     multiply_half(i - 1, half)

@@ -27,11 +27,16 @@ TILES = TOKENS // P
 PAIR = 2
 ROUND = 4
 ROUNDS = TILES // ROUND
-LOAD_AHEAD = 4
+LOAD_AHEAD = 10
+GROUP_SIZES = (4, 4, 2, 2, 2, 1, 1)
+LONGEST_GROUP = max(GROUP_SIZES)
+GROUP_OF = [g for g, size in enumerate(GROUP_SIZES) for n in range(size)]
+GROUP_FIRST = [sum(GROUP_SIZES[:g]) for g in range(len(GROUP_SIZES))]
 ROPE_ROUNDS = 4
 WARM_FIRST = 5
 WARM_BETWEEN = 2
 GPSIMD_BLOCKS = 3
+LAST_GROUP = len(GROUP_SIZES) - 1
 LAST_HALF = (ROUNDS - 1, ROUND // PAIR - 1)
 
 FLOPS = 2 * TOKENS * K * COLS
@@ -54,6 +59,7 @@ def tile_jointattention_pa_t_kernel(
         mx_pool = ctx.enter_context(tc.tile_pool(name="mx", bufs=2 * ROUND // PAIR))
         table_pool = ctx.enter_context(tc.tile_pool(name="table", bufs=3))
         res_pool = ctx.enter_context(tc.tile_pool(name="res", bufs=3))
+        cross_pool = ctx.enter_context(tc.tile_pool(name="cross", bufs=3))
         xt_psum = ctx.enter_context(tc.psum_pool(name="xt_psum", bufs=ROUND))
         qk_psum = ctx.enter_context(tc.psum_pool(name="qk_psum", bufs=ROUND // PAIR))
         v_psum = ctx.enter_context(tc.psum_pool(name="v_psum", bufs=2))
@@ -63,6 +69,7 @@ def tile_jointattention_pa_t_kernel(
         mx_tiles = {}
         table_tiles = {}
         res_tiles = {}
+        group_tiles = {}
 
         def load_round(r, pieces):
             x_sb = x_pool.tile([P, ROUND, K], BF16, name="x_sb")
@@ -114,10 +121,12 @@ def tile_jointattention_pa_t_kernel(
 
         load_round(1, 1)
         load_rope_part()
-        for r in range(2, LOAD_AHEAD):
+        for r in range(2, ROPE_ROUNDS):
             load_round(r, 1)
         for part in range(1, ROUNDS // ROPE_ROUNDS):
             load_rope_part()
+        for r in range(ROPE_ROUNDS, LOAD_AHEAD):
+            load_round(r, 1)
 
         def transpose_half(r, half):
             words = x_tiles[r][:].bitcast(F32)
@@ -188,10 +197,16 @@ def tile_jointattention_pa_t_kernel(
 
         def open_results(r):
             qk_accs, v_acc = res_tiles[r]
-            res_qk = res_pool.tile([P, 2 * HEADS, ROUND, D], F32, name="res_qk")
-            res_v = res_pool.tile([P, HEADS, ROUND, D], F32, name="res_v")
-            cross = res_pool.tile([P, 2 * HEADS, ROUND, D], F32, name="cross")
-            nc.scalar.copy(out=res_v[:].rearrange("p h t d -> p t h d"), in_=v_acc[:])
+            g = GROUP_OF[r]
+            if r == GROUP_FIRST[g]:
+                res_qk = res_pool.tile([P, 2 * HEADS, LONGEST_GROUP * ROUND, D], F32, name="res_qk")
+                res_v = res_pool.tile([P, HEADS, LONGEST_GROUP * ROUND, D], F32, name="res_v")
+                group_tiles[g] = (res_qk, res_v)
+            first = (r - GROUP_FIRST[g]) * ROUND
+            res_qk = group_tiles[g][0][:, :, first : first + ROUND, :]
+            res_v = group_tiles[g][1][:, :, first : first + ROUND, :]
+            cross = cross_pool.tile([P, 2 * HEADS, ROUND, D], F32, name="cross")
+            nc.scalar.copy(out=res_v.rearrange("p h t d -> p t h d"), in_=v_acc[:])
             res_tiles[r] = [qk_accs, res_qk, res_v, cross]
 
         def rotate_half(r, half):
@@ -233,18 +248,23 @@ def tile_jointattention_pa_t_kernel(
                 op=ADD,
             )
 
-        def store_v(r):
-            tiles = slice(r * ROUND, (r + 1) * ROUND)
-            nc.sync.dma_start(out=out_v_v[:, :, tiles, :], in_=res_tiles[r][2][:])
+        def store_v(g):
+            count = GROUP_SIZES[g] * ROUND
+            first = GROUP_FIRST[g] * ROUND
+            for h in range(HEADS):
+                nc.sync.dma_start(
+                    out=out_v_v[:, h, first : first + count, :],
+                    in_=group_tiles[g][1][:, h, 0:count, :],
+                )
 
-        def store_qk(r, first, count):
-            tiles = slice(r * ROUND + first, r * ROUND + first + count)
-            kept = slice(first, first + count)
-            res_qk = res_tiles[r][1]
-            nc.sync.dma_start(out=out_q_v[:, :, tiles, :], in_=res_qk[:, 0:HEADS, kept, :])
-            nc.sync.dma_start(
-                out=out_k_v[:, :, tiles, :], in_=res_qk[:, HEADS : 2 * HEADS, kept, :]
-            )
+        def store_qk(g, skip, count):
+            first = GROUP_FIRST[g] * ROUND + skip
+            for block in range(2 * HEADS):
+                target = out_q_v if block < HEADS else out_k_v
+                nc.sync.dma_start(
+                    out=target[:, block % HEADS, first : first + count, :],
+                    in_=group_tiles[g][0][:, block, skip : skip + count, :],
+                )
 
         for i in range(ROUNDS + 1):
             if i + LOAD_AHEAD < ROUNDS:
@@ -272,13 +292,14 @@ def tile_jointattention_pa_t_kernel(
                             nc.vector, before[0], before[1], GPSIMD_BLOCKS, 2 * HEADS - GPSIMD_BLOCKS
                         )
                 if i == ROUNDS and half == 0:
-                    store_v(i - 2)
-                    store_qk(i - 2, 0, ROUND)
-                    store_v(i - 1)
+                    store_v(LAST_GROUP - 1)
+                    store_qk(LAST_GROUP - 1, 0, ROUND)
+                    store_v(LAST_GROUP)
             if i == ROUNDS:
-                store_qk(i - 1, 0, PAIR)
+                store_qk(LAST_GROUP, 0, PAIR)
                 add_products(nc.vector, i - 1, 1, 0, 2 * HEADS)
-                store_qk(i - 1, PAIR, PAIR)
-            if 2 <= i < ROUNDS:
-                store_v(i - 2)
-                store_qk(i - 2, 0, ROUND)
+                store_qk(LAST_GROUP, PAIR, PAIR)
+            if 2 <= i < ROUNDS and GROUP_OF[i - 1] != GROUP_OF[i - 2]:
+                g = GROUP_OF[i - 2]
+                store_v(g)
+                store_qk(g, 0, GROUP_SIZES[g] * ROUND)

@@ -32,6 +32,8 @@ GROUP_SIZES = (4, 4, 2, 2, 2, 1, 1)
 LONGEST_GROUP = max(GROUP_SIZES)
 GROUP_OF = [g for g, size in enumerate(GROUP_SIZES) for n in range(size)]
 GROUP_FIRST = [sum(GROUP_SIZES[:g]) for g in range(len(GROUP_SIZES))]
+STORE_TILES = 8
+SORT_FROM = 3
 ROPE_ROUNDS = 4
 WARM_FIRST = 5
 WARM_BETWEEN = 2
@@ -57,6 +59,7 @@ def tile_jointattention_pa_t_kernel(
         const = ctx.enter_context(tc.tile_pool(name="const", bufs=1))
         x_pool = ctx.enter_context(tc.tile_pool(name="x", bufs=LOAD_AHEAD + 2))
         mx_pool = ctx.enter_context(tc.tile_pool(name="mx", bufs=2 * ROUND // PAIR))
+        sort_pool = ctx.enter_context(tc.tile_pool(name="sort", bufs=2))
         table_pool = ctx.enter_context(tc.tile_pool(name="table", bufs=3))
         res_pool = ctx.enter_context(tc.tile_pool(name="res", bufs=3))
         cross_pool = ctx.enter_context(tc.tile_pool(name="cross", bufs=3))
@@ -66,6 +69,7 @@ def tile_jointattention_pa_t_kernel(
         ctx.enter_context(tc.manual_schedule())
 
         x_tiles = {}
+        sorted_tiles = {}
         mx_tiles = {}
         table_tiles = {}
         res_tiles = {}
@@ -128,6 +132,14 @@ def tile_jointattention_pa_t_kernel(
         for r in range(ROPE_ROUNDS, LOAD_AHEAD):
             load_round(r, 1)
 
+        def sort_words(r):
+            sorted_sb = sort_pool.tile([P, PASSES, 2, P], F32, name="sorted_sb")
+            words = x_tiles[r][:, ROUND - 1, :].bitcast(F32)
+            nc.scalar.copy(
+                out=sorted_sb[:], in_=words.rearrange("p (g n u) -> p g u n", g=PASSES, u=2)
+            )
+            sorted_tiles[r] = sorted_sb
+
         def transpose_half(r, half):
             words = x_tiles[r][:].bitcast(F32)
             grouped = mx_pool.tile(
@@ -138,11 +150,11 @@ def tile_jointattention_pa_t_kernel(
                 for g in range(PASSES):
                     for u in range(2):
                         first = g * (K // PASSES // 2) + u
-                        nc.tensor.transpose(
-                            xt[:, g, u, :],
-                            words[:, half * PAIR + j, first : first + 2 * P - 1 : 2],
-                            ident[:],
-                        )
+                        if r >= SORT_FROM and half * PAIR + j == ROUND - 1:
+                            source = sorted_tiles[r][:, g, u, :]
+                        else:
+                            source = words[:, half * PAIR + j, first : first + 2 * P - 1 : 2]
+                        nc.tensor.transpose(xt[:, g, u, :], source, ident[:])
                 nc.scalar.copy(
                     out=grouped[:, j].bitcast(F32),
                     in_=xt[:].rearrange("p g u r -> p g r u"),
@@ -248,23 +260,23 @@ def tile_jointattention_pa_t_kernel(
                 op=ADD,
             )
 
+        def store(target, source, block, first, skip, count):
+            heads = HEADS if count <= STORE_TILES else 1
+            for h in range(0, HEADS, heads):
+                nc.sync.dma_start(
+                    out=target[:, h : h + heads, first : first + count, :],
+                    in_=source[:, block + h : block + h + heads, skip : skip + count, :],
+                )
+
         def store_v(g):
             count = GROUP_SIZES[g] * ROUND
             first = GROUP_FIRST[g] * ROUND
-            for h in range(HEADS):
-                nc.sync.dma_start(
-                    out=out_v_v[:, h, first : first + count, :],
-                    in_=group_tiles[g][1][:, h, 0:count, :],
-                )
+            store(out_v_v, group_tiles[g][1], 0, first, 0, count)
 
         def store_qk(g, skip, count):
             first = GROUP_FIRST[g] * ROUND + skip
-            for block in range(2 * HEADS):
-                target = out_q_v if block < HEADS else out_k_v
-                nc.sync.dma_start(
-                    out=target[:, block % HEADS, first : first + count, :],
-                    in_=group_tiles[g][0][:, block, skip : skip + count, :],
-                )
+            store(out_q_v, group_tiles[g][0], 0, first, skip, count)
+            store(out_k_v, group_tiles[g][0], HEADS, first, skip, count)
 
         for i in range(ROUNDS + 1):
             if i + LOAD_AHEAD < ROUNDS:
@@ -277,6 +289,8 @@ def tile_jointattention_pa_t_kernel(
             for half in range(ROUND // PAIR):
                 if 1 <= i <= ROUNDS:
                     multiply_half(i - 1, half)
+            if SORT_FROM <= i + 1 < ROUNDS:
+                sort_words(i + 1)
             if i < ROUNDS:
                 make_tables(i)
             if 1 <= i <= ROUNDS:

@@ -37,7 +37,6 @@ SORT_FROM = 3
 ROPE_ROUNDS = 4
 WARM_FIRST = 5
 WARM_BETWEEN = 2
-GPSIMD_BLOCKS = 3
 LAST_GROUP = len(GROUP_SIZES) - 1
 LAST_HALF = (ROUNDS - 1, ROUND // PAIR - 1)
 
@@ -247,16 +246,15 @@ def tile_jointattention_pa_t_kernel(
                 op=MULT,
             )
             if (r, half) != LAST_HALF:
-                add_products(nc.gpsimd, r, half, 0, GPSIMD_BLOCKS)
+                add_products(nc.gpsimd, r, half)
 
-        def add_products(engine, r, half, first, count):
+        def add_products(engine, r, half):
             res_qk, cross = res_tiles[r][1], res_tiles[r][3]
             tiles = slice(half * PAIR, (half + 1) * PAIR)
-            blocks = slice(first, first + count)
             engine.tensor_tensor(
-                out=res_qk[:, blocks, tiles, :],
-                in0=res_qk[:, blocks, tiles, :],
-                in1=cross[:, blocks, tiles, :],
+                out=res_qk[:, :, tiles, :],
+                in0=res_qk[:, :, tiles, :],
+                in1=cross[:, :, tiles, :],
                 op=ADD,
             )
 
@@ -300,18 +298,13 @@ def tile_jointattention_pa_t_kernel(
                     quantise_half(i, half)
                 if 1 <= i <= ROUNDS:
                     rotate_half(i - 1, half)
-                    before = (i - 1, 0) if half == 1 else (i - 2, 1)
-                    if before[0] >= 0:
-                        add_products(
-                            nc.vector, before[0], before[1], GPSIMD_BLOCKS, 2 * HEADS - GPSIMD_BLOCKS
-                        )
                 if i == ROUNDS and half == 0:
                     store_v(LAST_GROUP - 1)
                     store_qk(LAST_GROUP - 1, 0, ROUND)
                     store_v(LAST_GROUP)
             if i == ROUNDS:
                 store_qk(LAST_GROUP, 0, PAIR)
-                add_products(nc.vector, i - 1, 1, 0, 2 * HEADS)
+                add_products(nc.vector, i - 1, 1)
                 store_qk(LAST_GROUP, PAIR, PAIR)
             if 2 <= i < ROUNDS and GROUP_OF[i - 1] != GROUP_OF[i - 2]:
                 g = GROUP_OF[i - 2]

@@ -34,6 +34,8 @@ GROUP_OF = [g for g, size in enumerate(GROUP_SIZES) for n in range(size)]
 GROUP_FIRST = [sum(GROUP_SIZES[:g]) for g in range(len(GROUP_SIZES))]
 STORE_TILES = 8
 SORT_FROM = 3
+SORTED = 2
+TABLE_STEPS = (0, 2, 6, 10)
 ROPE_ROUNDS = 4
 WARM_FIRST = 5
 WARM_BETWEEN = 2
@@ -58,31 +60,33 @@ def tile_jointattention_pa_t_kernel(
         const = ctx.enter_context(tc.tile_pool(name="const", bufs=1))
         x_pool = ctx.enter_context(tc.tile_pool(name="x", bufs=LOAD_AHEAD + 2))
         mx_pool = ctx.enter_context(tc.tile_pool(name="mx", bufs=2 * ROUND // PAIR))
-        sort_pool = ctx.enter_context(tc.tile_pool(name="sort", bufs=2))
-        table_pool = ctx.enter_context(tc.tile_pool(name="table", bufs=3))
+        sort_pool = ctx.enter_context(tc.tile_pool(name="sort", bufs=2 * SORTED))
         res_pool = ctx.enter_context(tc.tile_pool(name="res", bufs=3))
         cross_pool = ctx.enter_context(tc.tile_pool(name="cross", bufs=3))
         xt_psum = ctx.enter_context(tc.psum_pool(name="xt_psum", bufs=ROUND))
-        qk_psum = ctx.enter_context(tc.psum_pool(name="qk_psum", bufs=ROUND // PAIR))
-        v_psum = ctx.enter_context(tc.psum_pool(name="v_psum", bufs=2))
+        qk_psum = ctx.enter_context(tc.psum_pool(name="qk_psum", bufs=ROUND // PAIR + 1))
+        v_psum = ctx.enter_context(tc.psum_pool(name="v_psum", bufs=1))
         ctx.enter_context(tc.manual_schedule())
 
         x_tiles = {}
         sorted_tiles = {}
         mx_tiles = {}
-        table_tiles = {}
+        table_parts = {}
         res_tiles = {}
         group_tiles = {}
 
         def load_round(r, pieces):
-            x_sb = x_pool.tile([P, ROUND, K], BF16, name="x_sb")
             step = ROUND // pieces
-            for j in range(0, ROUND, step):
-                nc.sync.dma_start(
-                    out=x_sb[:, j : j + step, :],
-                    in_=img_v[:, r * ROUND + j : r * ROUND + j + step, :],
-                )
+            x_sb = x_pool.tile([P, ROUND, K], BF16, name="x_sb")
             x_tiles[r] = x_sb
+            for j in range(0, ROUND, step):
+                load_piece(r, j, step)
+
+        def load_piece(r, j, count):
+            nc.sync.dma_start(
+                out=x_tiles[r][:, j : j + count, :],
+                in_=img_v[:, r * ROUND + j : r * ROUND + j + count, :],
+            )
 
         idle_sb = const.tile([P, 4 * P], BF16)
         nc.vector.memset(idle_sb[:], 0.0)
@@ -101,6 +105,9 @@ def tile_jointattention_pa_t_kernel(
                 )
 
         keep_busy(WARM_FIRST)
+
+        x_tiles[1] = x_pool.tile([P, ROUND, K], BF16, name="x_sb")
+        load_piece(1, 0, PAIR)
 
         w_code_sb = const.tile([P, PASSES, 2 * COLS], U8, align_bytes=64)
         nc.sync.dma_start(
@@ -122,7 +129,7 @@ def tile_jointattention_pa_t_kernel(
             nc.sync.dma_start(out=rope_sb[:], in_=rope_v[:, first : first + ROPE_ROUNDS * ROUND, :])
             rope_parts.append(rope_sb)
 
-        load_round(1, 1)
+        load_piece(1, PAIR, ROUND - PAIR)
         load_rope_part()
         for r in range(2, ROPE_ROUNDS):
             load_round(r, 1)
@@ -131,13 +138,13 @@ def tile_jointattention_pa_t_kernel(
         for r in range(ROPE_ROUNDS, LOAD_AHEAD):
             load_round(r, 1)
 
-        def sort_words(r):
+        def sort_words(r, j):
             sorted_sb = sort_pool.tile([P, PASSES, 2, P], F32, name="sorted_sb")
-            words = x_tiles[r][:, ROUND - 1, :].bitcast(F32)
+            words = x_tiles[r][:, j, :].bitcast(F32)
             nc.scalar.copy(
                 out=sorted_sb[:], in_=words.rearrange("p (g n u) -> p g u n", g=PASSES, u=2)
             )
-            sorted_tiles[r] = sorted_sb
+            sorted_tiles[(r, j)] = sorted_sb
 
         def transpose_half(r, half):
             words = x_tiles[r][:].bitcast(F32)
@@ -149,8 +156,8 @@ def tile_jointattention_pa_t_kernel(
                 for g in range(PASSES):
                     for u in range(2):
                         first = g * (K // PASSES // 2) + u
-                        if r >= SORT_FROM and half * PAIR + j == ROUND - 1:
-                            source = sorted_tiles[r][:, g, u, :]
+                        if (r, half * PAIR + j) in sorted_tiles:
+                            source = sorted_tiles[(r, half * PAIR + j)][:, g, u, :]
                         else:
                             source = words[:, half * PAIR + j, first : first + 2 * P - 1 : 2]
                         nc.tensor.transpose(xt[:, g, u, :], source, ident[:])
@@ -171,18 +178,13 @@ def tile_jointattention_pa_t_kernel(
             )
             mx_tiles[(r, half)] = [codes, scales]
 
-        def make_tables(r):
-            t0 = (r % ROPE_ROUNDS) * ROUND
-            rope_pairs = rope_parts[r // ROPE_ROUNDS][:].rearrange(
-                "p t (i h) -> p t i h", h=2
-            )
-            signed_sin = table_pool.tile([P, ROUND, D], BF16, name="signed_sin")
+        def make_table(part):
+            rope_pairs = rope_parts[part][:].rearrange("p t (i h) -> p t i h", h=2)
+            signed_sin = const.tile([P, ROPE_ROUNDS * ROUND, D], BF16, name="table%d" % part)
             sin_pairs = signed_sin[:].rearrange("p t (i h) -> p t i h", h=2)
-            nc.scalar.mul(
-                out=sin_pairs[:, :, :, 0], in_=rope_pairs[:, t0 : t0 + ROUND, :, 1], mul=-1.0
-            )
-            nc.scalar.copy(out=sin_pairs[:, :, :, 1], in_=rope_pairs[:, t0 : t0 + ROUND, :, 1])
-            table_tiles[r] = signed_sin
+            nc.vector.tensor_scalar_mul(sin_pairs[:, :, :, 0], rope_pairs[:, :, :, 1], -1.0)
+            nc.vector.tensor_copy(out=sin_pairs[:, :, :, 1], in_=rope_pairs[:, :, :, 1])
+            table_parts[part] = signed_sin
 
         def multiply_half(r, half):
             if half == 0:
@@ -222,7 +224,7 @@ def tile_jointattention_pa_t_kernel(
 
         def rotate_half(r, half):
             qk_accs, res_qk, res_v, cross = res_tiles[r]
-            signed_sin = table_tiles[r]
+            signed_sin = table_parts[r // ROPE_ROUNDS]
             shape = [P, PAIR, 2 * HEADS, HALF_D, 2]
             tiles = slice(half * PAIR, (half + 1) * PAIR)
             listed = (r % ROPE_ROUNDS) * ROUND + half * PAIR
@@ -239,7 +241,7 @@ def tile_jointattention_pa_t_kernel(
             nc.vector.tensor_tensor(
                 out=cross[:, :, tiles, :].rearrange("p c t (i h) -> p t c i h", h=2),
                 in0=acc_pairs[:, :, :, :, ::-1],
-                in1=signed_sin[:, tiles, :]
+                in1=signed_sin[:, listed : listed + PAIR, :]
                 .rearrange("p t (i h) -> p t i h", h=2)
                 .unsqueeze(2)
                 .to_broadcast(shape),
@@ -288,14 +290,15 @@ def tile_jointattention_pa_t_kernel(
                 if 1 <= i <= ROUNDS:
                     multiply_half(i - 1, half)
             if SORT_FROM <= i + 1 < ROUNDS:
-                sort_words(i + 1)
-            if i < ROUNDS:
-                make_tables(i)
+                for j in range(ROUND - SORTED, ROUND):
+                    sort_words(i + 1, j)
             if 1 <= i <= ROUNDS:
                 open_results(i - 1)
             for half in range(ROUND // PAIR):
                 if i < ROUNDS:
                     quantise_half(i, half)
+                if half == 1 and i in TABLE_STEPS:
+                    make_table(TABLE_STEPS.index(i))
                 if 1 <= i <= ROUNDS:
                     rotate_half(i - 1, half)
                 if i == ROUNDS and half == 0:

@@ -34,7 +34,7 @@ GROUP_OF = [g for g, size in enumerate(GROUP_SIZES) for n in range(size)]
 GROUP_FIRST = [sum(GROUP_SIZES[:g]) for g in range(len(GROUP_SIZES))]
 STORE_TILES = 8
 SORT_FROM = 3
-SORTED = 2
+SORTED = 1
 TABLE_STEPS = (0, 2, 6, 10)
 ROPE_ROUNDS = 4
 WARM_FIRST = 5

@@ -28,14 +28,13 @@ PAIR = 2
 ROUND = 4
 ROUNDS = TILES // ROUND
 LOAD_AHEAD = 10
-GROUP_SIZES = (4, 4, 2, 2, 2, 1, 1)
+GROUP_SIZES = (4, 4, 3, 2, 1, 1, 1)
 LONGEST_GROUP = max(GROUP_SIZES)
 GROUP_OF = [g for g, size in enumerate(GROUP_SIZES) for n in range(size)]
 GROUP_FIRST = [sum(GROUP_SIZES[:g]) for g in range(len(GROUP_SIZES))]
 STORE_TILES = 8
-SORT_FROM = 3
+SORT_FROM = 4
 SORTED = 1
-TABLE_STEPS = (0, 2, 6, 10)
 ROPE_ROUNDS = 4
 WARM_FIRST = 5
 WARM_BETWEEN = 2
@@ -60,6 +59,7 @@ def tile_jointattention_pa_t_kernel(
         const = ctx.enter_context(tc.tile_pool(name="const", bufs=1))
         x_pool = ctx.enter_context(tc.tile_pool(name="x", bufs=LOAD_AHEAD + 2))
         mx_pool = ctx.enter_context(tc.tile_pool(name="mx", bufs=2 * ROUND // PAIR))
+        table_pool = ctx.enter_context(tc.tile_pool(name="table", bufs=3))
         sort_pool = ctx.enter_context(tc.tile_pool(name="sort", bufs=2 * SORTED))
         res_pool = ctx.enter_context(tc.tile_pool(name="res", bufs=3))
         cross_pool = ctx.enter_context(tc.tile_pool(name="cross", bufs=3))
@@ -71,7 +71,7 @@ def tile_jointattention_pa_t_kernel(
         x_tiles = {}
         sorted_tiles = {}
         mx_tiles = {}
-        table_parts = {}
+        table_tiles = {}
         res_tiles = {}
         group_tiles = {}
 
@@ -129,8 +129,8 @@ def tile_jointattention_pa_t_kernel(
             nc.sync.dma_start(out=rope_sb[:], in_=rope_v[:, first : first + ROPE_ROUNDS * ROUND, :])
             rope_parts.append(rope_sb)
 
-        load_piece(1, PAIR, ROUND - PAIR)
         load_rope_part()
+        load_piece(1, PAIR, ROUND - PAIR)
         for r in range(2, ROPE_ROUNDS):
             load_round(r, 1)
         for part in range(1, ROUNDS // ROPE_ROUNDS):
@@ -178,13 +178,18 @@ def tile_jointattention_pa_t_kernel(
             )
             mx_tiles[(r, half)] = [codes, scales]
 
-        def make_table(part):
-            rope_pairs = rope_parts[part][:].rearrange("p t (i h) -> p t i h", h=2)
-            signed_sin = const.tile([P, ROPE_ROUNDS * ROUND, D], BF16, name="table%d" % part)
+        def make_tables(r):
+            t0 = (r % ROPE_ROUNDS) * ROUND
+            rope_pairs = rope_parts[r // ROPE_ROUNDS][:].rearrange(
+                "p t (i h) -> p t i h", h=2
+            )
+            signed_sin = table_pool.tile([P, ROUND, D], BF16, name="signed_sin")
             sin_pairs = signed_sin[:].rearrange("p t (i h) -> p t i h", h=2)
-            nc.vector.tensor_scalar_mul(sin_pairs[:, :, :, 0], rope_pairs[:, :, :, 1], -1.0)
-            nc.vector.tensor_copy(out=sin_pairs[:, :, :, 1], in_=rope_pairs[:, :, :, 1])
-            table_parts[part] = signed_sin
+            nc.scalar.mul(
+                out=sin_pairs[:, :, :, 0], in_=rope_pairs[:, t0 : t0 + ROUND, :, 1], mul=-1.0
+            )
+            nc.scalar.copy(out=sin_pairs[:, :, :, 1], in_=rope_pairs[:, t0 : t0 + ROUND, :, 1])
+            table_tiles[r] = signed_sin
 
         def multiply_half(r, half):
             if half == 0:
@@ -224,7 +229,7 @@ def tile_jointattention_pa_t_kernel(
 
         def rotate_half(r, half):
             qk_accs, res_qk, res_v, cross = res_tiles[r]
-            signed_sin = table_parts[r // ROPE_ROUNDS]
+            signed_sin = table_tiles[r]
             shape = [P, PAIR, 2 * HEADS, HALF_D, 2]
             tiles = slice(half * PAIR, (half + 1) * PAIR)
             listed = (r % ROPE_ROUNDS) * ROUND + half * PAIR
@@ -241,7 +246,7 @@ def tile_jointattention_pa_t_kernel(
             nc.vector.tensor_tensor(
                 out=cross[:, :, tiles, :].rearrange("p c t (i h) -> p t c i h", h=2),
                 in0=acc_pairs[:, :, :, :, ::-1],
-                in1=signed_sin[:, listed : listed + PAIR, :]
+                in1=signed_sin[:, tiles, :]
                 .rearrange("p t (i h) -> p t i h", h=2)
                 .unsqueeze(2)
                 .to_broadcast(shape),
@@ -278,38 +283,67 @@ def tile_jointattention_pa_t_kernel(
             store(out_q_v, group_tiles[g][0], 0, first, skip, count)
             store(out_k_v, group_tiles[g][0], HEADS, first, skip, count)
 
-        for i in range(ROUNDS + 1):
+        transpose_half(0, 0)
+        quantise_half(0, 0)
+        transpose_half(0, 1)
+        quantise_half(0, 1)
+        keep_busy(WARM_BETWEEN)
+        load_round(LOAD_AHEAD, 1)
+
+        transpose_half(1, 0)
+        make_tables(0)
+        multiply_half(0, 0)
+        multiply_half(0, 1)
+        open_results(0)
+        transpose_half(1, 1)
+        make_tables(1)
+        quantise_half(1, 0)
+        rotate_half(0, 0)
+        rotate_half(0, 1)
+        quantise_half(1, 1)
+        load_round(LOAD_AHEAD + 1, 1)
+
+        multiply_half(1, 0)
+        transpose_half(2, 0)
+        transpose_half(2, 1)
+        multiply_half(1, 1)
+        make_tables(2)
+        open_results(1)
+        rotate_half(1, 0)
+        quantise_half(2, 0)
+        rotate_half(1, 1)
+        quantise_half(2, 1)
+        load_round(LOAD_AHEAD + 2, 1)
+
+        for i in range(3, ROUNDS + 1):
             if i + LOAD_AHEAD < ROUNDS:
                 load_round(i + LOAD_AHEAD, 1)
-            for half in range(ROUND // PAIR):
-                if i < ROUNDS:
-                    transpose_half(i, half)
-            if i == 0:
-                keep_busy(WARM_BETWEEN)
-            for half in range(ROUND // PAIR):
-                if 1 <= i <= ROUNDS:
-                    multiply_half(i - 1, half)
+            if i < ROUNDS:
+                transpose_half(i, 0)
+                transpose_half(i, 1)
+            multiply_half(i - 1, 0)
+            multiply_half(i - 1, 1)
             if SORT_FROM <= i + 1 < ROUNDS:
                 for j in range(ROUND - SORTED, ROUND):
                     sort_words(i + 1, j)
-            if 1 <= i <= ROUNDS:
-                open_results(i - 1)
+            if i < ROUNDS:
+                make_tables(i)
+            open_results(i - 1)
             for half in range(ROUND // PAIR):
                 if i < ROUNDS:
                     quantise_half(i, half)
-                if half == 1 and i in TABLE_STEPS:
-                    make_table(TABLE_STEPS.index(i))
-                if 1 <= i <= ROUNDS:
-                    rotate_half(i - 1, half)
+                rotate_half(i - 1, half)
                 if i == ROUNDS and half == 0:
-                    store_v(LAST_GROUP - 1)
-                    store_qk(LAST_GROUP - 1, 0, ROUND)
                     store_v(LAST_GROUP)
+                    store_qk(LAST_GROUP - 1, PAIR, PAIR)
+            if i < ROUNDS and GROUP_OF[i - 1] != GROUP_OF[i - 2]:
+                g = GROUP_OF[i - 2]
+                store_v(g)
+                store_qk(g, 0, GROUP_SIZES[g] * ROUND)
+            if i == ROUNDS - 1:
+                store_v(LAST_GROUP - 1)
+                store_qk(LAST_GROUP - 1, 0, PAIR)
             if i == ROUNDS:
                 store_qk(LAST_GROUP, 0, PAIR)
                 add_products(nc.vector, i - 1, 1)
                 store_qk(LAST_GROUP, PAIR, PAIR)
-            if 2 <= i < ROUNDS and GROUP_OF[i - 1] != GROUP_OF[i - 2]:
-                g = GROUP_OF[i - 2]
-                store_v(g)
-                store_qk(g, 0, GROUP_SIZES[g] * ROUND)

from contextlib import ExitStack

import concourse.mybir as mybir
from concourse.masks import make_identity

BF16 = mybir.dt.bfloat16
F32 = mybir.dt.float32
I32 = mybir.dt.int32
U8 = mybir.dt.uint8
U32 = mybir.dt.uint32
FP8X4 = mybir.dt.float8_e4m3fn_x4
FP4X4 = mybir.dt.float4_e2m1fn_x4
MULT = mybir.AluOpType.mult
ADD = mybir.AluOpType.add

P = 128
TOKENS = 8192
K = 1024
PACK = 4
PASSES = K // (P * PACK)
HEADS = 2
D = 64
HALF_D = D // 2
COLS = 3 * HEADS * D
BLOCK = HEADS * D
TILES = TOKENS // P
PAIR = 2
ROUND = 4
ROUNDS = TILES // ROUND
LOAD_AHEAD = 10
GROUP_SIZES = (4, 4, 3, 2, 1, 1, 1)
LONGEST_GROUP = max(GROUP_SIZES)
GROUP_OF = [g for g, size in enumerate(GROUP_SIZES) for n in range(size)]
GROUP_FIRST = [sum(GROUP_SIZES[:g]) for g in range(len(GROUP_SIZES))]
STORE_TILES = 8
SORT_FROM = 4
SORTED = 1
ROPE_ROUNDS = 4
WARM_FIRST = 5
WARM_BETWEEN = 2
LAST_GROUP = len(GROUP_SIZES) - 1
LAST_HALF = (ROUNDS - 1, ROUND // PAIR - 1)

FLOPS = 2 * TOKENS * K * COLS


def tile_jointattention_pa_t_kernel(
    tc, img, rope, w_words, w_scales, out_q, out_k, out_v
):
    nc = tc.nc

    img_v = img.rearrange("b (p t) k -> p (b t) k", t=TILES)
    rope_v = rope.rearrange("b (p t) d -> p (b t) d", t=TILES)
    out_q_v = out_q.rearrange("b h (p t) d -> p (b h) t d", t=TILES)
    out_k_v = out_k.rearrange("b h (p t) d -> p (b h) t d", t=TILES)
    out_v_v = out_v.rearrange("b h (p t) d -> p (b h) t d", t=TILES)

    with ExitStack() as ctx:
        const = ctx.enter_context(tc.tile_pool(name="const", bufs=1))
        x_pool = ctx.enter_context(tc.tile_pool(name="x", bufs=LOAD_AHEAD + 2))
        mx_pool = ctx.enter_context(tc.tile_pool(name="mx", bufs=2 * ROUND // PAIR))
        table_pool = ctx.enter_context(tc.tile_pool(name="table", bufs=3))
        sort_pool = ctx.enter_context(tc.tile_pool(name="sort", bufs=2 * SORTED))
        res_pool = ctx.enter_context(tc.tile_pool(name="res", bufs=3))
        cross_pool = ctx.enter_context(tc.tile_pool(name="cross", bufs=3))
        xt_psum = ctx.enter_context(tc.psum_pool(name="xt_psum", bufs=ROUND))
        qk_psum = ctx.enter_context(tc.psum_pool(name="qk_psum", bufs=ROUND // PAIR + 1))
        v_psum = ctx.enter_context(tc.psum_pool(name="v_psum", bufs=1))
        ctx.enter_context(tc.manual_schedule())

        x_tiles = {}
        sorted_tiles = {}
        mx_tiles = {}
        table_tiles = {}
        res_tiles = {}
        group_tiles = {}

        def load_round(r, pieces):
            step = ROUND // pieces
            x_sb = x_pool.tile([P, ROUND, K], BF16, name="x_sb")
            x_tiles[r] = x_sb
            for j in range(0, ROUND, step):
                load_piece(r, j, step)

        def load_piece(r, j, count):
            nc.sync.dma_start(
                out=x_tiles[r][:, j : j + count, :],
                in_=img_v[:, r * ROUND + j : r * ROUND + j + count, :],
            )

        idle_sb = const.tile([P, 4 * P], BF16)
        nc.vector.memset(idle_sb[:], 0.0)
        w_scale_sb = const.tile([P, PASSES, COLS], U8, align_bytes=64)
        nc.vector.memset(w_scale_sb[:].bitcast(I32), 0)
        ident = const.tile([P, P], F32)
        make_identity(nc, ident[:])

        load_round(0, ROUND)

        def keep_busy(count):
            idle_acc = v_psum.tile([P, 4 * P], F32, name="v_acc")
            for n in range(count):
                nc.tensor.matmul(
                    idle_acc[:], lhsT=idle_sb[:, 0:P], rhs=idle_sb[:], start=True, stop=True
                )

        keep_busy(WARM_FIRST)

        x_tiles[1] = x_pool.tile([P, ROUND, K], BF16, name="x_sb")
        load_piece(1, 0, PAIR)

        w_code_sb = const.tile([P, PASSES, 2 * COLS], U8, align_bytes=64)
        nc.sync.dma_start(
            out=w_code_sb[:].bitcast(I32),
            in_=w_words.rearrange("g p b -> p g b").bitcast(I32),
        )
        for quad in range(4):
            nc.sync.dma_start(
                out=w_scale_sb[32 * quad : 32 * quad + 4].bitcast(I32),
                in_=w_scales[:, 4 * quad : 4 * quad + 4, :]
                .rearrange("g r n -> r g n")
                .bitcast(I32),
            )
        rope_parts = []

        def load_rope_part():
            first = len(rope_parts) * ROPE_ROUNDS * ROUND
            rope_sb = const.tile([P, ROPE_ROUNDS * ROUND, D], BF16, name="rope%d" % len(rope_parts))
            nc.sync.dma_start(out=rope_sb[:], in_=rope_v[:, first : first + ROPE_ROUNDS * ROUND, :])
            rope_parts.append(rope_sb)

        load_rope_part()
        load_piece(1, PAIR, ROUND - PAIR)
        for r in range(2, ROPE_ROUNDS):
            load_round(r, 1)
        for part in range(1, ROUNDS // ROPE_ROUNDS):
            load_rope_part()
        for r in range(ROPE_ROUNDS, LOAD_AHEAD):
            load_round(r, 1)

        def sort_words(r, j):
            sorted_sb = sort_pool.tile([P, PASSES, 2, P], F32, name="sorted_sb")
            words = x_tiles[r][:, j, :].bitcast(F32)
            nc.scalar.copy(
                out=sorted_sb[:], in_=words.rearrange("p (g n u) -> p g u n", g=PASSES, u=2)
            )
            sorted_tiles[(r, j)] = sorted_sb

        def transpose_half(r, half):
            words = x_tiles[r][:].bitcast(F32)
            grouped = mx_pool.tile(
                [P, PAIR, PASSES, P, PACK], BF16, align_bytes=64, name="grouped"
            )
            for j in range(PAIR):
                xt = xt_psum.tile([P, PASSES, 2, P], F32, name="xt")
                for g in range(PASSES):
                    for u in range(2):
                        first = g * (K // PASSES // 2) + u
                        if (r, half * PAIR + j) in sorted_tiles:
                            source = sorted_tiles[(r, half * PAIR + j)][:, g, u, :]
                        else:
                            source = words[:, half * PAIR + j, first : first + 2 * P - 1 : 2]
                        nc.tensor.transpose(xt[:, g, u, :], source, ident[:])
                nc.scalar.copy(
                    out=grouped[:, j].bitcast(F32),
                    in_=xt[:].rearrange("p g u r -> p g r u"),
                )
            mx_tiles[(r, half)] = [grouped]

        def quantise_half(r, half):
            grouped = mx_tiles[(r, half)][0]
            codes = mx_pool.tile([P, PAIR, PASSES, P], U32, align_bytes=64, name="codes")
            scales = mx_pool.tile([P, PAIR, PASSES, P], U8, align_bytes=64, name="scales")
            nc.vector.quantize_mx(
                out=codes[:].rearrange("p j g r -> p (j g r)").bitcast(FP8X4),
                scales=scales[:].rearrange("p j g r -> p (j g r)"),
                in_=grouped[:].rearrange("p j g r t -> p (j g r t)"),
            )
            mx_tiles[(r, half)] = [codes, scales]

        def make_tables(r):
            t0 = (r % ROPE_ROUNDS) * ROUND
            rope_pairs = rope_parts[r // ROPE_ROUNDS][:].rearrange(
                "p t (i h) -> p t i h", h=2
            )
            signed_sin = table_pool.tile([P, ROUND, D], BF16, name="signed_sin")
            sin_pairs = signed_sin[:].rearrange("p t (i h) -> p t i h", h=2)
            nc.scalar.mul(
                out=sin_pairs[:, :, :, 0], in_=rope_pairs[:, t0 : t0 + ROUND, :, 1], mul=-1.0
            )
            nc.scalar.copy(out=sin_pairs[:, :, :, 1], in_=rope_pairs[:, t0 : t0 + ROUND, :, 1])
            table_tiles[r] = signed_sin

        def multiply_half(r, half):
            if half == 0:
                v_acc = v_psum.tile([P, ROUND, HEADS, D], F32, name="v_acc")
                res_tiles[r] = [[], v_acc]
            qk_accs, v_acc = res_tiles[r]
            codes, scales = mx_tiles[(r, half)]
            qk_acc = qk_psum.tile([P, PAIR, 2 * HEADS, D], F32, name="qk_acc")
            qk_accs.append(qk_acc)
            products = [(j, c, qk_acc[:, j, HEADS * c : HEADS * (c + 1), :]) for j in range(PAIR) for c in range(2)]
            products.extend([(j, 2, v_acc[:, half * PAIR + j, :, :]) for j in range(PAIR)])
            for j, c, target in products:
                for g in range(PASSES):
                    nc.tensor.matmul_mx(
                        out=target.rearrange("p h d -> p (h d)"),
                        lhsT=codes[:, j, g, :].bitcast(FP8X4),
                        lhsT_scale=scales[:, j, g, :],
                        rhs=w_code_sb[:, g, 2 * BLOCK * c : 2 * BLOCK * (c + 1)].bitcast(FP4X4),
                        rhs_scale=w_scale_sb[:, g, BLOCK * c : BLOCK * (c + 1)],
                        start=(g == 0),
                        stop=(g == PASSES - 1),
                    )

        def open_results(r):
            qk_accs, v_acc = res_tiles[r]
            g = GROUP_OF[r]
            if r == GROUP_FIRST[g]:
                res_qk = res_pool.tile([P, 2 * HEADS, LONGEST_GROUP * ROUND, D], F32, name="res_qk")
                res_v = res_pool.tile([P, HEADS, LONGEST_GROUP * ROUND, D], F32, name="res_v")
                group_tiles[g] = (res_qk, res_v)
            first = (r - GROUP_FIRST[g]) * ROUND
            res_qk = group_tiles[g][0][:, :, first : first + ROUND, :]
            res_v = group_tiles[g][1][:, :, first : first + ROUND, :]
            cross = cross_pool.tile([P, 2 * HEADS, ROUND, D], F32, name="cross")
            nc.scalar.copy(out=res_v.rearrange("p h t d -> p t h d"), in_=v_acc[:])
            res_tiles[r] = [qk_accs, res_qk, res_v, cross]

        def rotate_half(r, half):
            qk_accs, res_qk, res_v, cross = res_tiles[r]
            signed_sin = table_tiles[r]
            shape = [P, PAIR, 2 * HEADS, HALF_D, 2]
            tiles = slice(half * PAIR, (half + 1) * PAIR)
            listed = (r % ROPE_ROUNDS) * ROUND + half * PAIR
            acc_pairs = qk_accs[half][:].rearrange("p t c (i h) -> p t c i h", h=2)
            nc.vector.tensor_tensor(
                out=res_qk[:, :, tiles, :].rearrange("p c t (i h) -> p c t i h", h=2),
                in0=acc_pairs.rearrange("p t c i h -> p c t i h"),
                in1=rope_parts[r // ROPE_ROUNDS][:, listed : listed + PAIR, :]
                .rearrange("p t (i h) -> p t i h", h=2)[:, :, :, 0:1]
                .unsqueeze(1)
                .to_broadcast([P, 2 * HEADS, PAIR, HALF_D, 2]),
                op=MULT,
            )
            nc.vector.tensor_tensor(
                out=cross[:, :, tiles, :].rearrange("p c t (i h) -> p t c i h", h=2),
                in0=acc_pairs[:, :, :, :, ::-1],
                in1=signed_sin[:, tiles, :]
                .rearrange("p t (i h) -> p t i h", h=2)
                .unsqueeze(2)
                .to_broadcast(shape),
                op=MULT,
            )
            if (r, half) != LAST_HALF:
                add_products(nc.gpsimd, r, half)

        def add_products(engine, r, half):
            res_qk, cross = res_tiles[r][1], res_tiles[r][3]
            tiles = slice(half * PAIR, (half + 1) * PAIR)
            engine.tensor_tensor(
                out=res_qk[:, :, tiles, :],
                in0=res_qk[:, :, tiles, :],
                in1=cross[:, :, tiles, :],
                op=ADD,
            )

        def store(target, source, block, first, skip, count):
            heads = HEADS if count <= STORE_TILES else 1
            for h in range(0, HEADS, heads):
                nc.sync.dma_start(
                    out=target[:, h : h + heads, first : first + count, :],
                    in_=source[:, block + h : block + h + heads, skip : skip + count, :],
                )

        def store_v(g):
            count = GROUP_SIZES[g] * ROUND
            first = GROUP_FIRST[g] * ROUND
            store(out_v_v, group_tiles[g][1], 0, first, 0, count)

        def store_qk(g, skip, count):
            first = GROUP_FIRST[g] * ROUND + skip
            store(out_q_v, group_tiles[g][0], 0, first, skip, count)
            store(out_k_v, group_tiles[g][0], HEADS, first, skip, count)

        transpose_half(0, 0)
        quantise_half(0, 0)
        transpose_half(0, 1)
        quantise_half(0, 1)
        keep_busy(WARM_BETWEEN)
        load_round(LOAD_AHEAD, 1)

        transpose_half(1, 0)
        make_tables(0)
        multiply_half(0, 0)
        multiply_half(0, 1)
        open_results(0)
        transpose_half(1, 1)
        make_tables(1)
        quantise_half(1, 0)
        rotate_half(0, 0)
        rotate_half(0, 1)
        quantise_half(1, 1)
        load_round(LOAD_AHEAD + 1, 1)

        multiply_half(1, 0)
        transpose_half(2, 0)
        transpose_half(2, 1)
        multiply_half(1, 1)
        make_tables(2)
        open_results(1)
        rotate_half(1, 0)
        quantise_half(2, 0)
        rotate_half(1, 1)
        quantise_half(2, 1)
        load_round(LOAD_AHEAD + 2, 1)

        for i in range(3, ROUNDS + 1):
            if i + LOAD_AHEAD < ROUNDS:
                load_round(i + LOAD_AHEAD, 1)
            if i < ROUNDS:
                transpose_half(i, 0)
                transpose_half(i, 1)
            multiply_half(i - 1, 0)
            multiply_half(i - 1, 1)
            if SORT_FROM <= i + 1 < ROUNDS:
                for j in range(ROUND - SORTED, ROUND):
                    sort_words(i + 1, j)
            if i < ROUNDS:
                make_tables(i)
            open_results(i - 1)
            for half in range(ROUND // PAIR):
                if i < ROUNDS:
                    quantise_half(i, half)
                rotate_half(i - 1, half)
                if i == ROUNDS and half == 0:
                    store_v(LAST_GROUP)
                    store_qk(LAST_GROUP - 1, PAIR, PAIR)
            if i < ROUNDS and GROUP_OF[i - 1] != GROUP_OF[i - 2]:
                g = GROUP_OF[i - 2]
                store_v(g)
                store_qk(g, 0, GROUP_SIZES[g] * ROUND)
            if i == ROUNDS - 1:
                store_v(LAST_GROUP - 1)
                store_qk(LAST_GROUP - 1, 0, PAIR)
            if i == ROUNDS:
                store_qk(LAST_GROUP, 0, PAIR)
                add_products(nc.vector, i - 1, 1)
                store_qk(LAST_GROUP, PAIR, PAIR)
